import numpy as np
import ml_dtypes


def mxq(x, axis, fmt="e4m3"):
    dtype, down = {"e4m3": (ml_dtypes.float8_e4m3fn, 7), "e5m2": (ml_dtypes.float8_e5m2, 14)}[fmt]
    v = np.moveaxis(np.asarray(x, np.float32).astype(ml_dtypes.bfloat16).astype(np.float64), axis, -1)
    blocks = v.reshape(v.shape[:-1] + (-1, 32))
    amax = np.abs(blocks).max(-1, keepdims=True)
    byte = np.maximum(np.where(amax > 0, np.frexp(amax)[1] - 1 + 127, 0) - down, 1)
    scale = np.exp2(byte - 127.0)
    codes = (blocks / scale).astype(np.float32).astype(dtype).astype(np.float64)
    return np.moveaxis((codes * scale).reshape(v.shape), -1, axis)


WIDE = False


def mx_kscale(k):
    if not WIDE:
        return np.ones(k)
    levels = np.array([10, -10, 5, -5, 0])
    a = np.random.permutation(np.resize(levels, k // 512 * 4)).reshape(k // 512, 4)
    idx = np.arange(k)
    return np.exp2(a[idx // 512, idx % 128 // 32])


BF16 = ml_dtypes.bfloat16


def bf(x):
    return np.asarray(x, np.float32).astype(BF16)


def f64(x):
    return np.asarray(x).astype(np.float64)


B, D_IN, HID, OUT = 8192, 512, 512, 128


def setup_inputs():
    s, t = mx_kscale(D_IN), mx_kscale(HID)
    u = np.concatenate([s, t])
    return {"x": bf(np.random.standard_normal((B, D_IN)) * s),
            "W1": bf(np.random.standard_normal((HID, D_IN)) / np.sqrt(D_IN) / s[None, :] * t[:, None]),
            "b1": bf(np.random.standard_normal(HID) * 0.3 * t),
            "W2": bf(np.random.standard_normal((OUT, D_IN + HID)) / np.sqrt(D_IN + HID) / u[None, :]),
            "b2": bf(np.random.standard_normal(OUT) * 0.3)}


def reference(x, W1, b1, W2, b2):
    xq = mxq(f64(x), 1, "e4m3")
    h1 = np.maximum((xq @ mxq(f64(W1), 1, "e4m3").T) + f64(b1), 0.0)
    concat = np.concatenate([xq, mxq(h1, 1, "e4m3")], axis=1)
    return (concat @ mxq(f64(W2), 1, "e4m3").T) + f64(b2)

@@ -1,0 +1,239 @@
+from contextlib import ExitStack
+
+import concourse.mybir as mybir
+from concourse.masks import make_identity
+
+F32 = mybir.dt.float32
+BF16 = mybir.dt.bfloat16
+U32 = mybir.dt.uint32
+U8 = mybir.dt.uint8
+FP8X4 = mybir.dt.float8_e4m3fn_x4
+RELU = mybir.ActivationFunctionType.Relu
+ADD = mybir.AluOpType.add
+
+P = 128
+B, D_IN, HID, OUT = 8192, 512, 512, 128
+GROUP = 512
+N_GROUPS = B // GROUP
+FLOPS = 2 * B * D_IN * HID + 2 * B * (D_IN + HID) * OUT
+
+VECTOR_TAKES_B = (0, 1, 2, 3, 4, 5, 7)
+
+
+def tile_dpn_t_kernel(tc, x, W1, b1, W2, b2, out):
+    nc = tc.nc
+    with ExitStack() as ctx:
+        const = ctx.enter_context(tc.tile_pool(name="const", bufs=1))
+        xin = ctx.enter_context(tc.tile_pool(name="xin", bufs=1))
+        xq = ctx.enter_context(tc.tile_pool(name="xq", bufs=1))
+        work = ctx.enter_context(tc.tile_pool(name="work", bufs=3))
+        outp = ctx.enter_context(tc.tile_pool(name="outp", bufs=4))
+        psum = ctx.enter_context(tc.psum_pool(name="psum", bufs=1))
+        ctx.enter_context(tc.manual_schedule())
+
+        ident = const.tile([P, P], F32, name="ident")
+        make_identity(nc, ident[:])
+        warm = const.tile([P, 1], F32, name="warm")
+        nc.vector.memset(warm[:], 0.0)
+        nc.scalar.activation(out=warm[:], in_=warm[:], func=RELU)
+
+        x_sb = [xin.tile([P, 4, D_IN], BF16, name="x%d" % g) for g in range(N_GROUPS)]
+        w1_sb = const.tile([P, 4, D_IN], BF16, name="w1_sb")
+        w2_sb = const.tile([P, D_IN + HID], BF16, name="w2_sb")
+        b1_raw = const.tile([P, 4], BF16, name="b1_raw")
+        b1_f = const.tile([P, 4], F32, name="b1_f")
+        b2_raw = const.tile([P, OUT], BF16, name="b2_raw")
+        b2_f = const.tile([P, OUT], F32, name="b2_f")
+
+        def load_x(g):
+            rows = x[g * GROUP : (g + 1) * GROUP, :]
+            nc.sync.dma_start(out=x_sb[g][:], in_=rows.rearrange("(p j) k -> p j k", j=4))
+
+        load_x(0)
+        nc.sync.dma_start(out=w1_sb[:], in_=W1.rearrange("(p t) k -> p t k", t=4))
+        nc.sync.dma_start(out=b1_raw[:], in_=b1.rearrange("(p t) -> p t", t=4))
+        load_x(1)
+        nc.sync.dma_start(out=w2_sb[:], in_=W2)
+        load_x(2)
+        nc.sync.dma_start(out=b2_raw[:], in_=b2.partition_broadcast(P))
+        for g in range(3, N_GROUPS):
+            load_x(g)
+        nc.gpsimd.tensor_copy(out=b1_f[:], in_=b1_raw[:])
+        nc.gpsimd.tensor_copy(out=b2_f[:], in_=b2_raw[:])
+
+        w1_g = const.tile([P, HID, 4], BF16, name="w1_g", align_bytes=64)
+        w1_c = const.tile([P, HID], U32, name="w1_c", align_bytes=64)
+        w1_s = const.tile([P, HID], U8, name="w1_s", align_bytes=64)
+        w2_g = const.tile([P, 2 * OUT, 4], BF16, name="w2_g", align_bytes=64)
+        w2_c = const.tile([P, 2 * OUT], U32, name="w2_c", align_bytes=64)
+        w2_s = const.tile([P, 2 * OUT], U8, name="w2_s", align_bytes=64)
+
+        def transpose_half(src, half, bank):
+            words = src[:].bitcast(F32)
+            for jj in range(2):
+                for u in range(2):
+                    nc.tensor.transpose(
+                        out=bank[:, jj, u, :],
+                        in_=words[:, 2 * half + jj, u * P : (u + 1) * P],
+                        identity=ident[:],
+                    )
+
+        def leave_bank(on_vector, bank, grouped, first_col):
+            dst = grouped[:].bitcast(F32)[:, first_col : first_col + 2 * P, :]
+            dst = dst.rearrange("p (j r) u -> p j r u", j=2)
+            src = bank[:].rearrange("p j u r -> p j r u")
+            if on_vector:
+                nc.vector.tensor_copy(out=dst, in_=src)
+            else:
+                nc.scalar.copy(out=dst, in_=src)
+
+        def quantise(grouped, codes, scales):
+            nc.vector.quantize_mx(
+                out=codes[:].bitcast(FP8X4),
+                scales=scales[:],
+                in_=grouped[:].rearrange("p w j -> p (w j)"),
+            )
+
+        live = {}
+
+        def st_transpose(g):
+            for half, tag in ((0, "xa"), (1, "xb")):
+                bank = psum.tile([P, 2, 2, P], F32, name="%s%d" % (tag, g), tag=tag)
+                live[(tag, g)] = bank
+                transpose_half(x_sb[g], half, bank)
+
+        def st_leave_x(g):
+            grouped = work.tile([P, GROUP, 4], BF16, name="xg%d" % g, tag="xg", align_bytes=64)
+            live[("xg", g)] = grouped
+            leave_bank(False, live[("xa", g)], grouped, 0)
+            leave_bank(g in VECTOR_TAKES_B, live[("xb", g)], grouped, 2 * P)
+
+        def st_quantise_x(g):
+            codes = xq.tile([P, GROUP], U32, name="xc%d" % g, align_bytes=64)
+            scales = xq.tile([P, GROUP], U8, name="xs%d" % g, align_bytes=64)
+            live[("xc", g)] = codes
+            live[("xs", g)] = scales
+            quantise(live[("xg", g)], codes, scales)
+
+        def st_mm1(g, t):
+            z = psum.tile([P, GROUP], F32, name="z%d_%d" % (t, g), tag="z%d" % t)
+            live[("z", g, t)] = z
+            nc.tensor.matmul_mx(
+                out=z[:],
+                lhsT=w1_c[:, t * P : (t + 1) * P].bitcast(FP8X4),
+                lhsT_scale=w1_s[:, t * P : (t + 1) * P],
+                rhs=live[("xc", g)][:].bitcast(FP8X4),
+                rhs_scale=live[("xs", g)][:],
+                start=True,
+                stop=True,
+            )
+
+        def st_relu(g, t):
+            if t == 0:
+                live[("hp", g)] = work.tile([P, 4, GROUP], BF16, name="hp%d" % g, tag="hp")
+            nc.scalar.activation(
+                out=live[("hp", g)][:, t, :],
+                in_=live[("z", g, t)][:],
+                func=RELU,
+                bias=b1_f[:, t : t + 1],
+                scale=1.0,
+            )
+
+        def st_regroup(g):
+            grouped = work.tile([P, GROUP, 4], BF16, name="hg%d" % g, tag="hg", align_bytes=64)
+            live[("hg", g)] = grouped
+            nc.vector.tensor_copy(
+                out=grouped[:].rearrange("p (c i) t -> p c t i", i=4),
+                in_=live[("hp", g)][:].rearrange("p t (c i) -> p c t i", i=4),
+            )
+
+        def st_quantise_h(g):
+            codes = work.tile([P, GROUP], U32, name="hc%d" % g, tag="hc", align_bytes=64)
+            scales = work.tile([P, GROUP], U8, name="hs%d" % g, tag="hs", align_bytes=64)
+            live[("hc", g)] = codes
+            live[("hs", g)] = scales
+            quantise(live[("hg", g)], codes, scales)
+
+        def st_mm2(g):
+            acc = psum.tile([P, 4, OUT], F32, name="o%d" % g, tag="o", bufs=2)
+            live[("o", g)] = acc
+            for j in range(4):
+                cols = slice(j * P, (j + 1) * P)
+                nc.tensor.matmul_mx(
+                    out=acc[:, j, :],
+                    lhsT=live[("xc", g)][:, cols].bitcast(FP8X4),
+                    lhsT_scale=live[("xs", g)][:, cols],
+                    rhs=w2_c[:, 0:OUT].bitcast(FP8X4),
+                    rhs_scale=w2_s[:, 0:OUT],
+                    start=True,
+                    stop=False,
+                )
+                nc.tensor.matmul_mx(
+                    out=acc[:, j, :],
+                    lhsT=live[("hc", g)][:, cols].bitcast(FP8X4),
+                    lhsT_scale=live[("hs", g)][:, cols],
+                    rhs=w2_c[:, OUT : 2 * OUT].bitcast(FP8X4),
+                    rhs_scale=w2_s[:, OUT : 2 * OUT],
+                    start=False,
+                    stop=True,
+                )
+
+        def st_out(g):
+            res = outp.tile([P, 4, OUT], F32, name="res%d" % g, tag="res")
+            nc.vector.tensor_tensor(
+                out=res[:],
+                in0=live[("o", g)][:],
+                in1=b2_f[:].unsqueeze(1).to_broadcast([P, 4, OUT]),
+                op=ADD,
+            )
+            rows = out[g * GROUP : (g + 1) * GROUP, :]
+            nc.sync.dma_start(out=rows.rearrange("(p j) o -> p j o", j=4), in_=res[:])
+
+        def prepare_w1():
+            banks = []
+            for half in range(2):
+                bank = psum.tile([P, 2, 2, P], F32, name="w1b%d" % half, tag="z%d" % half)
+                banks.append(bank)
+                transpose_half(w1_sb, half, bank)
+            leave_bank(False, banks[0], w1_g, 0)
+            leave_bank(True, banks[1], w1_g, 2 * P)
+
+        def prepare_w2():
+            bank = psum.tile([P, 2, 2, P], F32, name="w2b", tag="z2")
+            words = w2_sb[:].bitcast(F32)
+            for u in range(2):
+                nc.tensor.transpose(out=bank[:, 0, u, :], in_=words[:, u * P : (u + 1) * P], identity=ident[:])
+            for v in range(2):
+                nc.tensor.transpose(out=bank[:, 1, v, :], in_=words[:, 2 * P + v : 4 * P : 2], identity=ident[:])
+            leave_bank(True, bank, w2_g, 0)
+            quantise(w2_g, w2_c, w2_s)
+
+        def has(g):
+            return 0 <= g < N_GROUPS
+
+        for n in range(-2, N_GROUPS + 3):
+            if has(n + 2):
+                st_transpose(n + 2)
+            if n == -2:
+                st_leave_x(0)
+                prepare_w1()
+            if has(n + 1):
+                st_quantise_x(n + 1)
+            if n == -1:
+                quantise(w1_g, w1_c, w1_s)
+                prepare_w2()
+            if has(n - 1):
+                st_quantise_h(n - 1)
+            if has(n - 2):
+                st_mm2(n - 2)
+            for t in range(4):
+                if has(n):
+                    st_relu(n, t)
+                if has(n + 1):
+                    st_mm1(n + 1, t)
+            if has(n + 2) and n != -2:
+                st_leave_x(n + 2)
+            if has(n - 2):
+                st_out(n - 2)
+            if has(n):
+                st_regroup(n)

@@ -17,7 +17,7 @@ GROUP = 512
 N_GROUPS = B // GROUP
 FLOPS = 2 * B * D_IN * HID + 2 * B * (D_IN + HID) * OUT
 
-VECTOR_TAKES_B = (0, 1, 2, 3, 4, 5, 7)
+VECTOR_TAKES_B = (0, 1, 2, 4, 6, 8, 10, 12)
 
 
 def tile_dpn_t_kernel(tc, x, W1, b1, W2, b2, out):
@@ -49,14 +49,17 @@ def tile_dpn_t_kernel(tc, x, W1, b1, W2, b2, out):
             rows = x[g * GROUP : (g + 1) * GROUP, :]
             nc.sync.dma_start(out=x_sb[g][:], in_=rows.rearrange("(p j) k -> p j k", j=4))
 
+        w1_rows = W1.rearrange("(p t) k -> p t k", t=4)
         load_x(0)
-        nc.sync.dma_start(out=w1_sb[:], in_=W1.rearrange("(p t) k -> p t k", t=4))
+        nc.sync.dma_start(out=w1_sb[:, 0:2, :], in_=w1_rows[:, 0:2, :])
+        nc.sync.dma_start(out=w1_sb[:, 2:4, :], in_=w1_rows[:, 2:4, :])
         nc.sync.dma_start(out=b1_raw[:], in_=b1.rearrange("(p t) -> p t", t=4))
         load_x(1)
-        nc.sync.dma_start(out=w2_sb[:], in_=W2)
         load_x(2)
+        nc.sync.dma_start(out=w2_sb[:], in_=W2)
+        load_x(3)
         nc.sync.dma_start(out=b2_raw[:], in_=b2.partition_broadcast(P))
-        for g in range(3, N_GROUPS):
+        for g in range(4, N_GROUPS):
             load_x(g)
         nc.gpsimd.tensor_copy(out=b1_f[:], in_=b1_raw[:])
         nc.gpsimd.tensor_copy(out=b2_f[:], in_=b2_raw[:])
@@ -89,9 +92,9 @@ def tile_dpn_t_kernel(tc, x, W1, b1, W2, b2, out):
 
         def quantise(grouped, codes, scales):
             nc.vector.quantize_mx(
-                out=codes[:].bitcast(FP8X4),
-                scales=scales[:],
-                in_=grouped[:].rearrange("p w j -> p (w j)"),
+                out=codes.bitcast(FP8X4),
+                scales=scales,
+                in_=grouped.rearrange("p w j -> p (w j)"),
             )
 
         live = {}
@@ -113,7 +116,7 @@ def tile_dpn_t_kernel(tc, x, W1, b1, W2, b2, out):
             scales = xq.tile([P, GROUP], U8, name="xs%d" % g, align_bytes=64)
             live[("xc", g)] = codes
             live[("xs", g)] = scales
-            quantise(live[("xg", g)], codes, scales)
+            quantise(live[("xg", g)][:], codes[:], scales[:])
 
         def st_mm1(g, t):
             z = psum.tile([P, GROUP], F32, name="z%d_%d" % (t, g), tag="z%d" % t)
@@ -152,7 +155,7 @@ def tile_dpn_t_kernel(tc, x, W1, b1, W2, b2, out):
             scales = work.tile([P, GROUP], U8, name="hs%d" % g, tag="hs", align_bytes=64)
             live[("hc", g)] = codes
             live[("hs", g)] = scales
-            quantise(live[("hg", g)], codes, scales)
+            quantise(live[("hg", g)][:], codes[:], scales[:])
 
         def st_mm2(g):
             acc = psum.tile([P, 4, OUT], F32, name="o%d" % g, tag="o", bufs=2)
@@ -189,41 +192,52 @@ def tile_dpn_t_kernel(tc, x, W1, b1, W2, b2, out):
             rows = out[g * GROUP : (g + 1) * GROUP, :]
             nc.sync.dma_start(out=rows.rearrange("(p j) o -> p j o", j=4), in_=res[:])
 
-        def prepare_w1():
-            banks = []
-            for half in range(2):
-                bank = psum.tile([P, 2, 2, P], F32, name="w1b%d" % half, tag="z%d" % half)
-                banks.append(bank)
-                transpose_half(w1_sb, half, bank)
-            leave_bank(False, banks[0], w1_g, 0)
-            leave_bank(True, banks[1], w1_g, 2 * P)
+        def prepare_w1(half, on_vector):
+            bank = psum.tile([P, 2, 2, P], F32, name="w1b%d" % half, tag="z%d" % half)
+            transpose_half(w1_sb, half, bank)
+            leave_bank(on_vector, bank, w1_g, half * 2 * P)
 
-        def prepare_w2():
-            bank = psum.tile([P, 2, 2, P], F32, name="w2b", tag="z2")
+        def quantise_w1(half):
+            cols = slice(half * 2 * P, (half + 1) * 2 * P)
+            quantise(w1_g[:, cols, :], w1_c[:, cols], w1_s[:, cols])
+
+        def transpose_w2():
+            bank = psum.tile([P, 2, 2, P], F32, name="w2b", tag="o", bufs=2)
+            live["w2b"] = bank
             words = w2_sb[:].bitcast(F32)
             for u in range(2):
                 nc.tensor.transpose(out=bank[:, 0, u, :], in_=words[:, u * P : (u + 1) * P], identity=ident[:])
             for v in range(2):
                 nc.tensor.transpose(out=bank[:, 1, v, :], in_=words[:, 2 * P + v : 4 * P : 2], identity=ident[:])
-            leave_bank(True, bank, w2_g, 0)
-            quantise(w2_g, w2_c, w2_s)
 
         def has(g):
             return 0 <= g < N_GROUPS
 
-        for n in range(-2, N_GROUPS + 3):
+        st_transpose(0)
+        st_leave_x(0)
+        prepare_w1(0, True)
+        prepare_w1(1, False)
+        st_quantise_x(0)
+        quantise_w1(0)
+        quantise_w1(1)
+        st_transpose(1)
+        st_leave_x(1)
+        for t in range(4):
+            st_mm1(0, t)
+
+        for n in range(N_GROUPS + 3):
             if has(n + 2):
                 st_transpose(n + 2)
-            if n == -2:
-                st_leave_x(0)
-                prepare_w1()
+            if n == 0:
+                transpose_w2()
             if has(n + 1):
                 st_quantise_x(n + 1)
-            if n == -1:
-                quantise(w1_g, w1_c, w1_s)
-                prepare_w2()
+            if n == 0:
+                leave_bank(True, live["w2b"], w2_g, 0)
             if has(n - 1):
                 st_quantise_h(n - 1)
+            if n == 0:
+                quantise(w2_g[:], w2_c[:], w2_s[:])
             if has(n - 2):
                 st_mm2(n - 2)
             for t in range(4):
@@ -231,7 +245,7 @@ def tile_dpn_t_kernel(tc, x, W1, b1, W2, b2, out):
                     st_relu(n, t)
                 if has(n + 1):
                     st_mm1(n + 1, t)
-            if has(n + 2) and n != -2:
+            if has(n + 2):
                 st_leave_x(n + 2)
             if has(n - 2):
                 st_out(n - 2)

@@ -17,7 +17,11 @@ GROUP = 512
 N_GROUPS = B // GROUP
 FLOPS = 2 * B * D_IN * HID + 2 * B * (D_IN + HID) * OUT
 
-VECTOR_TAKES_B = (0, 1, 2, 4, 6, 8, 10, 12)
+VECTOR_TAKES = ((0,1),(1,1),(2,0),(2,1),(5,1),(8,1),(11,1))
+LAST = (256,256)
+DIRECT = ()
+SREGROUP = (16,)
+UNITS = [(g, 0, GROUP) for g in range(N_GROUPS - 1)] + [(N_GROUPS - 1, sum(LAST[:k]), LAST[k]) for k in range(len(LAST))]
 
 
 def tile_dpn_t_kernel(tc, x, W1, b1, W2, b2, out):
@@ -25,17 +29,14 @@ def tile_dpn_t_kernel(tc, x, W1, b1, W2, b2, out):
     with ExitStack() as ctx:
         const = ctx.enter_context(tc.tile_pool(name="const", bufs=1))
         xin = ctx.enter_context(tc.tile_pool(name="xin", bufs=1))
-        xq = ctx.enter_context(tc.tile_pool(name="xq", bufs=1))
-        work = ctx.enter_context(tc.tile_pool(name="work", bufs=3))
+        work = ctx.enter_context(tc.tile_pool(name="work", bufs=4))
+        codes_pool = ctx.enter_context(tc.tile_pool(name="codes", bufs=7))
         outp = ctx.enter_context(tc.tile_pool(name="outp", bufs=4))
         psum = ctx.enter_context(tc.psum_pool(name="psum", bufs=1))
         ctx.enter_context(tc.manual_schedule())
 
         ident = const.tile([P, P], F32, name="ident")
         make_identity(nc, ident[:])
-        warm = const.tile([P, 1], F32, name="warm")
-        nc.vector.memset(warm[:], 0.0)
-        nc.scalar.activation(out=warm[:], in_=warm[:], func=RELU)
 
         x_sb = [xin.tile([P, 4, D_IN], BF16, name="x%d" % g) for g in range(N_GROUPS)]
         w1_sb = const.tile([P, 4, D_IN], BF16, name="w1_sb")
@@ -45,22 +46,28 @@ def tile_dpn_t_kernel(tc, x, W1, b1, W2, b2, out):
         b2_raw = const.tile([P, OUT], BF16, name="b2_raw")
         b2_f = const.tile([P, OUT], F32, name="b2_f")
 
-        def load_x(g):
-            rows = x[g * GROUP : (g + 1) * GROUP, :]
-            nc.sync.dma_start(out=x_sb[g][:], in_=rows.rearrange("(p j) k -> p j k", j=4))
+        def load_x(g, first, count):
+            rows = x[g * GROUP : (g + 1) * GROUP, :].rearrange("(p j) k -> p j k", j=4)
+            slots = slice(first, first + count)
+            nc.sync.dma_start(out=x_sb[g][:, slots, :], in_=rows[:, slots, :])
 
         w1_rows = W1.rearrange("(p t) k -> p t k", t=4)
-        load_x(0)
+        nc.scalar.dma_start(out=b1_raw[:], in_=b1.rearrange("(p t) -> p t", t=4))
+        warm = const.tile([P, 1], F32, name="warm")
+        nc.vector.memset(warm[:], 0.0)
+        nc.scalar.activation(out=warm[:], in_=warm[:], func=RELU)
+        load_x(0, 0, 2)
+        load_x(0, 2, 2)
         nc.sync.dma_start(out=w1_sb[:, 0:2, :], in_=w1_rows[:, 0:2, :])
         nc.sync.dma_start(out=w1_sb[:, 2:4, :], in_=w1_rows[:, 2:4, :])
-        nc.sync.dma_start(out=b1_raw[:], in_=b1.rearrange("(p t) -> p t", t=4))
-        load_x(1)
-        load_x(2)
+        load_x(1, 0, 2)
+        load_x(1, 2, 2)
         nc.sync.dma_start(out=w2_sb[:], in_=W2)
-        load_x(3)
+        load_x(2, 0, 4)
+        load_x(3, 0, 4)
         nc.sync.dma_start(out=b2_raw[:], in_=b2.partition_broadcast(P))
         for g in range(4, N_GROUPS):
-            load_x(g)
+            load_x(g, 0, 4)
         nc.gpsimd.tensor_copy(out=b1_f[:], in_=b1_raw[:])
         nc.gpsimd.tensor_copy(out=b2_f[:], in_=b2_raw[:])
 
@@ -71,9 +78,11 @@ def tile_dpn_t_kernel(tc, x, W1, b1, W2, b2, out):
         w2_c = const.tile([P, 2 * OUT], U32, name="w2_c", align_bytes=64)
         w2_s = const.tile([P, 2 * OUT], U8, name="w2_s", align_bytes=64)
 
-        def transpose_half(src, half, bank):
+        live = {}
+
+        def transpose_half(src, half, bank, slots=(0, 1)):
             words = src[:].bitcast(F32)
-            for jj in range(2):
+            for jj in slots:
                 for u in range(2):
                     nc.tensor.transpose(
                         out=bank[:, jj, u, :],
@@ -81,9 +90,8 @@ def tile_dpn_t_kernel(tc, x, W1, b1, W2, b2, out):
                         identity=ident[:],
                     )
 
-        def leave_bank(on_vector, bank, grouped, first_col):
-            dst = grouped[:].bitcast(F32)[:, first_col : first_col + 2 * P, :]
-            dst = dst.rearrange("p (j r) u -> p j r u", j=2)
+        def leave_bank(on_vector, bank, dst):
+            dst = dst.bitcast(F32).rearrange("p (j r) u -> p j r u", j=2)
             src = bank[:].rearrange("p j u r -> p j r u")
             if on_vector:
                 nc.vector.tensor_copy(out=dst, in_=src)
@@ -97,75 +105,109 @@ def tile_dpn_t_kernel(tc, x, W1, b1, W2, b2, out):
                 in_=grouped.rearrange("p w j -> p (w j)"),
             )
 
-        live = {}
+        def has(n):
+            return 0 <= n < len(UNITS)
 
-        def st_transpose(g):
-            for half, tag in ((0, "xa"), (1, "xb")):
-                bank = psum.tile([P, 2, 2, P], F32, name="%s%d" % (tag, g), tag=tag)
-                live[(tag, g)] = bank
-                transpose_half(x_sb[g], half, bank)
+        def st_transpose(g, half):
+            bank = psum.tile([P, 2, 2, P], F32, name="x%d_%d" % (half, g), tag="x%d" % half)
+            live[("x", g, half)] = bank
+            transpose_half(x_sb[g], half, bank)
 
-        def st_leave_x(g):
-            grouped = work.tile([P, GROUP, 4], BF16, name="xg%d" % g, tag="xg", align_bytes=64)
-            live[("xg", g)] = grouped
-            leave_bank(False, live[("xa", g)], grouped, 0)
-            leave_bank(g in VECTOR_TAKES_B, live[("xb", g)], grouped, 2 * P)
+        def pair(m):
+            if ("pair", m) not in live:
+                x_width = GROUP if 0 <= m < N_GROUPS else 0
+                h_width = UNITS[m - 3][2] if has(m - 3) else 0
+                width = x_width + h_width
+                live[("pair", m)] = work.tile([P, width, 4], BF16, name="pair%d" % m, tag="pair", align_bytes=64)
+                live[("codes", m)] = codes_pool.tile([P, width], U32, name="c%d" % m, tag="c", align_bytes=64)
+                live[("scales", m)] = codes_pool.tile([P, width], U8, name="s%d" % m, tag="s", align_bytes=64)
+            return live[("pair", m)], (GROUP if m < N_GROUPS else 0)
 
-        def st_quantise_x(g):
-            codes = xq.tile([P, GROUP], U32, name="xc%d" % g, align_bytes=64)
-            scales = xq.tile([P, GROUP], U8, name="xs%d" % g, align_bytes=64)
-            live[("xc", g)] = codes
-            live[("xs", g)] = scales
-            quantise(live[("xg", g)][:], codes[:], scales[:])
+        def st_leave_x(g, half):
+            tile, h_first = pair(g)
+            first = half * 2 * P
+            leave_bank((g, half) in VECTOR_TAKES, live[("x", g, half)], tile[:, first : first + 2 * P, :])
 
-        def st_mm1(g, t):
-            z = psum.tile([P, GROUP], F32, name="z%d_%d" % (t, g), tag="z%d" % t)
-            live[("z", g, t)] = z
+        def st_quantise(m):
+            tile, h_first = pair(m)
+            quantise(tile[:], live[("codes", m)][:], live[("scales", m)][:])
+
+        def st_mm1(n, t):
+            g, first, width = UNITS[n]
+            if n in DIRECT:
+                z = psum.tile([P, 4, P], F32, name="zd%d_%d" % (t, n), tag="z%d" % t)
+                live[("z", n, t)] = z
+                for tt in range(4):
+                    nc.tensor.matmul_mx(
+                        out=z[:, tt, :],
+                        lhsT=w1_c[:, tt * P : (tt + 1) * P].bitcast(FP8X4),
+                        lhsT_scale=w1_s[:, tt * P : (tt + 1) * P],
+                        rhs=live[("codes", g)][:, t * P : (t + 1) * P].bitcast(FP8X4),
+                        rhs_scale=live[("scales", g)][:, t * P : (t + 1) * P],
+                        start=True,
+                        stop=True,
+                    )
+                return
+            cols = slice(first, first + width)
+            z = psum.tile([P, width], F32, name="z%d_%d" % (t, n), tag="z%d" % t)
+            live[("z", n, t)] = z
             nc.tensor.matmul_mx(
                 out=z[:],
                 lhsT=w1_c[:, t * P : (t + 1) * P].bitcast(FP8X4),
                 lhsT_scale=w1_s[:, t * P : (t + 1) * P],
-                rhs=live[("xc", g)][:].bitcast(FP8X4),
-                rhs_scale=live[("xs", g)][:],
+                rhs=live[("codes", g)][:, cols].bitcast(FP8X4),
+                rhs_scale=live[("scales", g)][:, cols],
                 start=True,
                 stop=True,
             )
 
-        def st_relu(g, t):
+        def st_relu(n, t):
+            width = UNITS[n][2]
+            if n in DIRECT:
+                tile, h_first = pair(n + 3)
+                nc.vector.tensor_tensor(
+                    out=tile[:, h_first + t * P : h_first + (t + 1) * P, :],
+                    in0=live[("z", n, t)][:].rearrange("p t c -> p c t"),
+                    in1=b1_f[:].unsqueeze(1).to_broadcast([P, P, 4]),
+                    op=ADD,
+                )
+                return
             if t == 0:
-                live[("hp", g)] = work.tile([P, 4, GROUP], BF16, name="hp%d" % g, tag="hp")
+                live[("hp", n)] = work.tile([P, 4, width], BF16, name="hp%d" % n, tag="hp")
             nc.scalar.activation(
-                out=live[("hp", g)][:, t, :],
-                in_=live[("z", g, t)][:],
+                out=live[("hp", n)][:, t, :],
+                in_=live[("z", n, t)][:],
                 func=RELU,
                 bias=b1_f[:, t : t + 1],
                 scale=1.0,
             )
 
-        def st_regroup(g):
-            grouped = work.tile([P, GROUP, 4], BF16, name="hg%d" % g, tag="hg", align_bytes=64)
-            live[("hg", g)] = grouped
-            nc.vector.tensor_copy(
-                out=grouped[:].rearrange("p (c i) t -> p c t i", i=4),
-                in_=live[("hp", g)][:].rearrange("p t (c i) -> p c t i", i=4),
-            )
+        def st_regroup(n):
+            width = UNITS[n][2]
+            tile, h_first = pair(n + 3)
+            if n in DIRECT:
+                whole = tile[:, h_first : h_first + width, :].rearrange("p c t -> p (c t)")
+                nc.vector.tensor_scalar_max(out=whole, in0=whole, scalar1=0.0)
+                return
+            dst = tile[:, h_first : h_first + width, :].rearrange("p (c i) t -> p c t i", i=4)
+            src = live[("hp", n)][:].rearrange("p t (c i) -> p c t i", i=4)
+            if n in SREGROUP:
+                nc.scalar.copy(out=dst, in_=src)
+            else:
+                nc.vector.tensor_copy(out=dst, in_=src)
 
-        def st_quantise_h(g):
-            codes = work.tile([P, GROUP], U32, name="hc%d" % g, tag="hc", align_bytes=64)
-            scales = work.tile([P, GROUP], U8, name="hs%d" % g, tag="hs", align_bytes=64)
-            live[("hc", g)] = codes
-            live[("hs", g)] = scales
-            quantise(live[("hg", g)][:], codes[:], scales[:])
-
-        def st_mm2(g):
-            acc = psum.tile([P, 4, OUT], F32, name="o%d" % g, tag="o", bufs=2)
-            live[("o", g)] = acc
-            for j in range(4):
-                cols = slice(j * P, (j + 1) * P)
+        def st_mm2(n):
+            g, first, width = UNITS[n]
+            h_first = pair(n + 3)[1]
+            acc = psum.tile([P, width // P, OUT], F32, name="o%d" % n, tag="o", bufs=2)
+            live[("o", n)] = acc
+            for j in range(width // P):
+                x_cols = slice(first + j * P, first + (j + 1) * P)
+                h_cols = slice(h_first + j * P, h_first + (j + 1) * P)
                 nc.tensor.matmul_mx(
                     out=acc[:, j, :],
-                    lhsT=live[("xc", g)][:, cols].bitcast(FP8X4),
-                    lhsT_scale=live[("xs", g)][:, cols],
+                    lhsT=live[("codes", g)][:, x_cols].bitcast(FP8X4),
+                    lhsT_scale=live[("scales", g)][:, x_cols],
                     rhs=w2_c[:, 0:OUT].bitcast(FP8X4),
                     rhs_scale=w2_s[:, 0:OUT],
                     start=True,
@@ -173,29 +215,31 @@ def tile_dpn_t_kernel(tc, x, W1, b1, W2, b2, out):
                 )
                 nc.tensor.matmul_mx(
                     out=acc[:, j, :],
-                    lhsT=live[("hc", g)][:, cols].bitcast(FP8X4),
-                    lhsT_scale=live[("hs", g)][:, cols],
+                    lhsT=live[("codes", n + 3)][:, h_cols].bitcast(FP8X4),
+                    lhsT_scale=live[("scales", n + 3)][:, h_cols],
                     rhs=w2_c[:, OUT : 2 * OUT].bitcast(FP8X4),
                     rhs_scale=w2_s[:, OUT : 2 * OUT],
                     start=False,
                     stop=True,
                 )
 
-        def st_out(g):
-            res = outp.tile([P, 4, OUT], F32, name="res%d" % g, tag="res")
+        def st_out(n):
+            g, first, width = UNITS[n]
+            slots = slice(first // P, (first + width) // P)
+            res = outp.tile([P, width // P, OUT], F32, name="res%d" % n, tag="res")
             nc.vector.tensor_tensor(
                 out=res[:],
-                in0=live[("o", g)][:],
-                in1=b2_f[:].unsqueeze(1).to_broadcast([P, 4, OUT]),
+                in0=live[("o", n)][:],
+                in1=b2_f[:].unsqueeze(1).to_broadcast([P, width // P, OUT]),
                 op=ADD,
             )
-            rows = out[g * GROUP : (g + 1) * GROUP, :]
-            nc.sync.dma_start(out=rows.rearrange("(p j) o -> p j o", j=4), in_=res[:])
+            rows = out[g * GROUP : (g + 1) * GROUP, :].rearrange("(p j) o -> p j o", j=4)
+            nc.sync.dma_start(out=rows[:, slots, :], in_=res[:])
 
         def prepare_w1(half, on_vector):
             bank = psum.tile([P, 2, 2, P], F32, name="w1b%d" % half, tag="z%d" % half)
             transpose_half(w1_sb, half, bank)
-            leave_bank(on_vector, bank, w1_g, half * 2 * P)
+            leave_bank(on_vector, bank, w1_g[:, half * 2 * P : (half + 1) * 2 * P, :])
 
         def quantise_w1(half):
             cols = slice(half * 2 * P, (half + 1) * 2 * P)
@@ -210,44 +254,50 @@ def tile_dpn_t_kernel(tc, x, W1, b1, W2, b2, out):
             for v in range(2):
                 nc.tensor.transpose(out=bank[:, 1, v, :], in_=words[:, 2 * P + v : 4 * P : 2], identity=ident[:])
 
-        def has(g):
-            return 0 <= g < N_GROUPS
+        def bring(g):
+            for half in range(2):
+                st_transpose(g, half)
+                st_leave_x(g, half)
 
-        st_transpose(0)
-        st_leave_x(0)
-        prepare_w1(0, True)
-        prepare_w1(1, False)
-        st_quantise_x(0)
+        N_UNITS = len(UNITS)
+        bring(0)
+        prepare_w1(0, 0 in ())
+        st_quantise(0)
         quantise_w1(0)
+        prepare_w1(1, 1 in ())
         quantise_w1(1)
-        st_transpose(1)
-        st_leave_x(1)
+        bring(1)
         for t in range(4):
             st_mm1(0, t)
+        st_quantise(1)
+        bring(2)
 
-        for n in range(N_GROUPS + 3):
-            if has(n + 2):
-                st_transpose(n + 2)
-            if n == 0:
-                transpose_w2()
-            if has(n + 1):
-                st_quantise_x(n + 1)
-            if n == 0:
-                leave_bank(True, live["w2b"], w2_g, 0)
-            if has(n - 1):
-                st_quantise_h(n - 1)
-            if n == 0:
-                quantise(w2_g[:], w2_c[:], w2_s[:])
-            if has(n - 2):
+        for n in range(0, N_UNITS + 3):
+            if n + 3 < N_GROUPS:
+                st_transpose(n + 3, 0)
+                st_transpose(n + 3, 1)
+            if has(n - 2) and n - 2 < N_UNITS - 1:
                 st_mm2(n - 2)
+            if n + 2 < N_GROUPS or has(n - 1):
+                st_quantise(n + 2)
+            if n == 1:
+                transpose_w2()
+                leave_bank(1, live["w2b"], w2_g[:])
+            if has(n - 1) and n - 1 >= N_UNITS - 1:
+                st_mm2(n - 1)
             for t in range(4):
                 if has(n):
                     st_relu(n, t)
                 if has(n + 1):
                     st_mm1(n + 1, t)
-            if has(n + 2):
-                st_leave_x(n + 2)
-            if has(n - 2):
-                st_out(n - 2)
+            if n + 3 < N_GROUPS:
+                st_leave_x(n + 3, 0)
+                st_leave_x(n + 3, 1)
+            if n == 1:
+                quantise(w2_g[:], w2_c[:], w2_s[:])
             if has(n):
                 st_regroup(n)
+            if has(n - 2) and n - 2 < N_UNITS - 1:
+                st_out(n - 2)
+            if has(n - 1) and n - 1 >= N_UNITS - 1:
+                st_out(n - 1)

@@ -10,6 +10,7 @@ U8 = mybir.dt.uint8
 FP8X4 = mybir.dt.float8_e4m3fn_x4
 RELU = mybir.ActivationFunctionType.Relu
 ADD = mybir.AluOpType.add
+MULT = mybir.AluOpType.mult
 
 P = 128
 B, D_IN, HID, OUT = 8192, 512, 512, 128
@@ -21,6 +22,10 @@ VECTOR_TAKES = ((0,1),(1,1),(2,0),(2,1),(5,1),(8,1),(11,1))
 LAST = (256,256)
 DIRECT = ()
 SREGROUP = (16,)
+GREGROUP = ()
+GPARTS = 1
+GSHARE = 64
+SHARED = ()
 UNITS = [(g, 0, GROUP) for g in range(N_GROUPS - 1)] + [(N_GROUPS - 1, sum(LAST[:k]), LAST[k]) for k in range(len(LAST))]
 
 
@@ -31,7 +36,7 @@ def tile_dpn_t_kernel(tc, x, W1, b1, W2, b2, out):
         xin = ctx.enter_context(tc.tile_pool(name="xin", bufs=1))
         work = ctx.enter_context(tc.tile_pool(name="work", bufs=4))
         codes_pool = ctx.enter_context(tc.tile_pool(name="codes", bufs=7))
-        outp = ctx.enter_context(tc.tile_pool(name="outp", bufs=4))
+        outp = ctx.enter_context(tc.tile_pool(name="outp", bufs=8))
         psum = ctx.enter_context(tc.psum_pool(name="psum", bufs=1))
         ctx.enter_context(tc.manual_schedule())
 
@@ -45,6 +50,8 @@ def tile_dpn_t_kernel(tc, x, W1, b1, W2, b2, out):
         b1_f = const.tile([P, 4], F32, name="b1_f")
         b2_raw = const.tile([P, OUT], BF16, name="b2_raw")
         b2_f = const.tile([P, OUT], F32, name="b2_f")
+        hold_h = const.tile([P, 1], BF16, name="hold_h")
+        hold = const.tile([P, 1], U32, name="hold")
 
         def load_x(g, first, count):
             rows = x[g * GROUP : (g + 1) * GROUP, :].rearrange("(p j) k -> p j k", j=4)
@@ -62,8 +69,9 @@ def tile_dpn_t_kernel(tc, x, W1, b1, W2, b2, out):
         nc.sync.dma_start(out=w1_sb[:, 2:4, :], in_=w1_rows[:, 2:4, :])
         load_x(1, 0, 2)
         load_x(1, 2, 2)
+        load_x(2, 0, 2)
+        load_x(2, 2, 2)
         nc.sync.dma_start(out=w2_sb[:], in_=W2)
-        load_x(2, 0, 4)
         load_x(3, 0, 4)
         nc.sync.dma_start(out=b2_raw[:], in_=b2.partition_broadcast(P))
         for g in range(4, N_GROUPS):
@@ -172,7 +180,7 @@ def tile_dpn_t_kernel(tc, x, W1, b1, W2, b2, out):
                     op=ADD,
                 )
                 return
-            if t == 0:
+            if ("hp", n) not in live:
                 live[("hp", n)] = work.tile([P, 4, width], BF16, name="hp%d" % n, tag="hp")
             nc.scalar.activation(
                 out=live[("hp", n)][:, t, :],
@@ -182,6 +190,11 @@ def tile_dpn_t_kernel(tc, x, W1, b1, W2, b2, out):
                 scale=1.0,
             )
 
+        def g_share(n):
+            if n in GREGROUP:
+                return UNITS[n][2]
+            return GSHARE if n in SHARED and n not in DIRECT else 0
+
         def st_regroup(n):
             width = UNITS[n][2]
             tile, h_first = pair(n + 3)
@@ -189,12 +202,38 @@ def tile_dpn_t_kernel(tc, x, W1, b1, W2, b2, out):
                 whole = tile[:, h_first : h_first + width, :].rearrange("p c t -> p (c t)")
                 nc.vector.tensor_scalar_max(out=whole, in0=whole, scalar1=0.0)
                 return
+            width -= g_share(n)
+            if width == 0:
+                return
             dst = tile[:, h_first : h_first + width, :].rearrange("p (c i) t -> p c t i", i=4)
-            src = live[("hp", n)][:].rearrange("p t (c i) -> p c t i", i=4)
+            src = live[("hp", n)][:, :, :width].rearrange("p t (c i) -> p c t i", i=4)
             if n in SREGROUP:
                 nc.scalar.copy(out=dst, in_=src)
             else:
                 nc.vector.tensor_copy(out=dst, in_=src)
+
+        def st_regroup_g(n):
+            width = UNITS[n][2]
+            share = g_share(n)
+            if share == 0:
+                return
+            tile, h_first = pair(n + 3)
+            if n in GREGROUP:
+                nc.gpsimd.tensor_copy(out=hold[:], in_=live[("codes", n + 2)][:, 0:1])
+            else:
+                nc.gpsimd.tensor_copy(out=hold_h[:], in_=tile[:, h_first, 0:1])
+            parts = GPARTS if n in GREGROUP else 1
+            step = share // parts
+            for k in range(parts):
+                cols = slice(width - share + k * step, width - share + (k + 1) * step)
+                nc.gpsimd.tensor_scalar(
+                    out=tile[:, h_first + cols.start : h_first + cols.stop, :],
+                    in0=live[("hp", n)][:, :, cols].rearrange("p t c -> p c t"),
+                    scalar1=1.0,
+                    scalar2=0.0,
+                    op0=MULT,
+                    op1=ADD,
+                )
 
         def st_mm2(n):
             g, first, width = UNITS[n]
@@ -272,32 +311,61 @@ def tile_dpn_t_kernel(tc, x, W1, b1, W2, b2, out):
         st_quantise(1)
         bring(2)
 
+        order = [0, 1, 2, 3]
+        halves = [0, 1]
         for n in range(0, N_UNITS + 3):
-            if n + 3 < N_GROUPS:
-                st_transpose(n + 3, 0)
-                st_transpose(n + 3, 1)
-            if has(n - 2) and n - 2 < N_UNITS - 1:
+            late_out = has(n - 2) and n - 2 < N_UNITS - 1
+            if late_out and False:
                 st_mm2(n - 2)
-            if n + 2 < N_GROUPS or has(n - 1):
-                st_quantise(n + 2)
+            if n + 3 < N_GROUPS:
+                for half in halves:
+                    st_transpose(n + 3, half)
+            mm2_last = True and has(n + 1) and n not in DIRECT
+            if late_out and not False and not mm2_last:
+                st_mm2(n - 2)
+            if late_out:
+                if False:
+                    st_out(n - 2)
+            if n in DIRECT:
+                for t in order:
+                    st_relu(n, t)
+                    if has(n + 1):
+                        st_mm1(n + 1, t)
+                if False:
+                    st_out(n - 2)
+                if False:
+                    st_regroup(n)
+            if False and (n + 3, 1) in VECTOR_TAKES:
+                st_leave_x(n + 3, 1)
             if n == 1:
-                transpose_w2()
+                if not True:
+                    transpose_w2()
                 leave_bank(1, live["w2b"], w2_g[:])
+            if n != 0 and (n + 2 < N_GROUPS or has(n - 1)):
+                st_quantise(n + 2)
             if has(n - 1) and n - 1 >= N_UNITS - 1:
                 st_mm2(n - 1)
-            for t in range(4):
+            for t in order if n not in DIRECT else ():
                 if has(n):
                     st_relu(n, t)
                 if has(n + 1):
                     st_mm1(n + 1, t)
+            if late_out and not False and mm2_last:
+                st_mm2(n - 2)
             if n + 3 < N_GROUPS:
-                st_leave_x(n + 3, 0)
-                st_leave_x(n + 3, 1)
+                for half in halves:
+                    if not (False and half == 1 and (n + 3, 1) in VECTOR_TAKES):
+                        st_leave_x(n + 3, half)
+            if has(n) and not (False and n in DIRECT):
+                st_regroup(n)
+                st_regroup_g(n)
+            if n == 0:
+                st_quantise(2)
+            if True and n == 1 - 1:
+                transpose_w2()
             if n == 1:
                 quantise(w2_g[:], w2_c[:], w2_s[:])
-            if has(n):
-                st_regroup(n)
-            if has(n - 2) and n - 2 < N_UNITS - 1:
+            if late_out and not False and not (False and n in DIRECT):
                 st_out(n - 2)
             if has(n - 1) and n - 1 >= N_UNITS - 1:
                 st_out(n - 1)

@@ -24,8 +24,9 @@ DIRECT = ()
 SREGROUP = (16,)
 GREGROUP = ()
 GPARTS = 1
-GSHARE = 64
-SHARED = ()
+GSHARE = 256
+EX = ()
+SHARED = tuple(n - 1 for n in EX) if GSHARE else ()
 UNITS = [(g, 0, GROUP) for g in range(N_GROUPS - 1)] + [(N_GROUPS - 1, sum(LAST[:k]), LAST[k]) for k in range(len(LAST))]
 
 
@@ -134,7 +135,7 @@ def tile_dpn_t_kernel(tc, x, W1, b1, W2, b2, out):
         def st_leave_x(g, half):
             tile, h_first = pair(g)
             first = half * 2 * P
-            leave_bank((g, half) in VECTOR_TAKES, live[("x", g, half)], tile[:, first : first + 2 * P, :])
+            leave_bank((g, half) in VECTOR_TAKES or g - 3 in EX, live[("x", g, half)], tile[:, first : first + 2 * P, :])
 
         def st_quantise(m):
             tile, h_first = pair(m)
@@ -208,7 +209,10 @@ def tile_dpn_t_kernel(tc, x, W1, b1, W2, b2, out):
             dst = tile[:, h_first : h_first + width, :].rearrange("p (c i) t -> p c t i", i=4)
             src = live[("hp", n)][:, :, :width].rearrange("p t (c i) -> p c t i", i=4)
             if n in SREGROUP:
-                nc.scalar.copy(out=dst, in_=src)
+                nc.scalar.copy(
+                    out=tile[:, h_first : h_first + width, :],
+                    in_=live[("hp", n)][:, :, :width].rearrange("p t c -> p c t"),
+                )
             else:
                 nc.vector.tensor_copy(out=dst, in_=src)
 
@@ -293,6 +297,34 @@ def tile_dpn_t_kernel(tc, x, W1, b1, W2, b2, out):
             for v in range(2):
                 nc.tensor.transpose(out=bank[:, 1, v, :], in_=words[:, 2 * P + v : 4 * P : 2], identity=ident[:])
 
+        def bring_slot(slot, tag, on_vector):
+            bank = psum.tile([P, 2, P], F32, name="x0s%d" % slot, tag=tag)
+            words = x_sb[0][:].bitcast(F32)
+            for u in range(2):
+                nc.tensor.transpose(out=bank[:, u, :], in_=words[:, slot, u * P : (u + 1) * P], identity=ident[:])
+            dst = pair(0)[0][:, slot * P : (slot + 1) * P, :].rearrange("p c j -> p (c j)").bitcast(F32).rearrange("p (r u) -> p r u", u=2)
+            src = bank[:].rearrange("p u r -> p r u")
+            if on_vector:
+                nc.vector.tensor_copy(out=dst, in_=src)
+            else:
+                nc.scalar.copy(out=dst, in_=src)
+
+        def bring_w1(t):
+            bank = psum.tile([P, 2, P], F32, name="w1q%d" % t, tag=("z0", "z1", "o", "o")[t], bufs=(1, 1, 2, 2)[t])
+            words = w1_sb[:].bitcast(F32)
+            for u in range(2):
+                nc.tensor.transpose(out=bank[:, u, :], in_=words[:, t, u * P : (u + 1) * P], identity=ident[:])
+            dst = w1_g[:, t * P : (t + 1) * P, :].rearrange("p c j -> p (c j)").bitcast(F32).rearrange("p (r u) -> p r u", u=2)
+            src = bank[:].rearrange("p u r -> p r u")
+            if t in ():
+                nc.vector.tensor_copy(out=dst, in_=src)
+            else:
+                nc.scalar.copy(out=dst, in_=src)
+
+        def quantise_w1q(first, count):
+            cols = slice(first * P, (first + count) * P)
+            quantise(w1_g[:, cols, :], w1_c[:, cols], w1_s[:, cols])
+
         def bring(g):
             for half in range(2):
                 st_transpose(g, half)
@@ -310,6 +342,8 @@ def tile_dpn_t_kernel(tc, x, W1, b1, W2, b2, out):
             st_mm1(0, t)
         st_quantise(1)
         bring(2)
+        transpose_w2()
+        leave_bank(True, live["w2b"], w2_g[:])
 
         order = [0, 1, 2, 3]
         halves = [0, 1]
@@ -320,7 +354,7 @@ def tile_dpn_t_kernel(tc, x, W1, b1, W2, b2, out):
             if n + 3 < N_GROUPS:
                 for half in halves:
                     st_transpose(n + 3, half)
-            mm2_last = True and has(n + 1) and n not in DIRECT
+            mm2_last = False and has(n + 1) and n not in DIRECT
             if late_out and not False and not mm2_last:
                 st_mm2(n - 2)
             if late_out:
@@ -335,9 +369,11 @@ def tile_dpn_t_kernel(tc, x, W1, b1, W2, b2, out):
                     st_out(n - 2)
                 if False:
                     st_regroup(n)
-            if False and (n + 3, 1) in VECTOR_TAKES:
-                st_leave_x(n + 3, 1)
-            if n == 1:
+            early = n in EX and n + 3 < N_GROUPS
+            if early:
+                for half in halves:
+                    st_leave_x(n + 3, half)
+            if n == 1 and not True:
                 if not True:
                     transpose_w2()
                 leave_bank(1, live["w2b"], w2_g[:])
@@ -346,7 +382,7 @@ def tile_dpn_t_kernel(tc, x, W1, b1, W2, b2, out):
             if has(n - 1) and n - 1 >= N_UNITS - 1:
                 st_mm2(n - 1)
             for t in order if n not in DIRECT else ():
-                if has(n):
+                if has(n) and (n != 0 or not False):
                     st_relu(n, t)
                 if has(n + 1):
                     st_mm1(n + 1, t)
@@ -354,14 +390,14 @@ def tile_dpn_t_kernel(tc, x, W1, b1, W2, b2, out):
                 st_mm2(n - 2)
             if n + 3 < N_GROUPS:
                 for half in halves:
-                    if not (False and half == 1 and (n + 3, 1) in VECTOR_TAKES):
+                    if not early:
                         st_leave_x(n + 3, half)
             if has(n) and not (False and n in DIRECT):
                 st_regroup(n)
                 st_regroup_g(n)
             if n == 0:
                 st_quantise(2)
-            if True and n == 1 - 1:
+            if True and not True and n == 1 - 1:
                 transpose_w2()
             if n == 1:
                 quantise(w2_g[:], w2_c[:], w2_s[:])

@@ -60,7 +60,7 @@ def tile_dpn_t_kernel(tc, x, W1, b1, W2, b2, out):
             nc.sync.dma_start(out=x_sb[g][:, slots, :], in_=rows[:, slots, :])
 
         w1_rows = W1.rearrange("(p t) k -> p t k", t=4)
-        nc.scalar.dma_start(out=b1_raw[:], in_=b1.rearrange("(p t) -> p t", t=4))
+
         warm = const.tile([P, 1], F32, name="warm")
         nc.vector.memset(warm[:], 0.0)
         nc.scalar.activation(out=warm[:], in_=warm[:], func=RELU)
@@ -68,14 +68,18 @@ def tile_dpn_t_kernel(tc, x, W1, b1, W2, b2, out):
         load_x(0, 2, 2)
         nc.sync.dma_start(out=w1_sb[:, 0:2, :], in_=w1_rows[:, 0:2, :])
         nc.sync.dma_start(out=w1_sb[:, 2:4, :], in_=w1_rows[:, 2:4, :])
+        nc.sync.dma_start(out=b1_raw[:], in_=b1.rearrange("(p t) -> p t", t=4))
         load_x(1, 0, 2)
         load_x(1, 2, 2)
         load_x(2, 0, 2)
         load_x(2, 2, 2)
         nc.sync.dma_start(out=w2_sb[:], in_=W2)
         load_x(3, 0, 4)
+        load_x(4, 0, 4)
+        load_x(5, 0, 4)
+        load_x(6, 0, 4)
         nc.sync.dma_start(out=b2_raw[:], in_=b2.partition_broadcast(P))
-        for g in range(4, N_GROUPS):
+        for g in range(7, N_GROUPS):
             load_x(g, 0, 4)
         nc.gpsimd.tensor_copy(out=b1_f[:], in_=b1_raw[:])
         nc.gpsimd.tensor_copy(out=b2_f[:], in_=b2_raw[:])

@@ -18,11 +18,11 @@ GROUP = 512
 N_GROUPS = B // GROUP
 FLOPS = 2 * B * D_IN * HID + 2 * B * (D_IN + HID) * OUT
 
-VECTOR_TAKES = ((0,1),(1,1),(2,0),(2,1),(5,1),(8,1),(11,1))
+VECTOR_TAKES = ((0,1),(2,0),(2,1))
 LAST = (256,256)
-DIRECT = ()
+DIRECT = (3,9)
 SREGROUP = (16,)
-GREGROUP = ()
+GREGROUP = (2,8)
 GPARTS = 1
 GSHARE = 256
 EX = ()
@@ -210,8 +210,8 @@ def tile_dpn_t_kernel(tc, x, W1, b1, W2, b2, out):
             width -= g_share(n)
             if width == 0:
                 return
-            dst = tile[:, h_first : h_first + width, :].rearrange("p (c i) t -> p c t i", i=4)
-            src = live[("hp", n)][:, :, :width].rearrange("p t (c i) -> p c t i", i=4)
+            dst = tile[:, h_first : h_first + width, :].rearrange("p (c i) t -> p c t i", i=8)
+            src = live[("hp", n)][:, :, :width].rearrange("p t (c i) -> p c t i", i=8)
             if n in SREGROUP:
                 nc.scalar.copy(
                     out=tile[:, h_first : h_first + width, :],
@@ -369,9 +369,9 @@ def tile_dpn_t_kernel(tc, x, W1, b1, W2, b2, out):
                     st_relu(n, t)
                     if has(n + 1):
                         st_mm1(n + 1, t)
-                if False:
+                if True:
                     st_out(n - 2)
-                if False:
+                if True:
                     st_regroup(n)
             early = n in EX and n + 3 < N_GROUPS
             if early:
@@ -396,7 +396,7 @@ def tile_dpn_t_kernel(tc, x, W1, b1, W2, b2, out):
                 for half in halves:
                     if not early:
                         st_leave_x(n + 3, half)
-            if has(n) and not (False and n in DIRECT):
+            if has(n) and not (True and n in DIRECT):
                 st_regroup(n)
                 st_regroup_g(n)
             if n == 0:
@@ -405,7 +405,7 @@ def tile_dpn_t_kernel(tc, x, W1, b1, W2, b2, out):
                 transpose_w2()
             if n == 1:
                 quantise(w2_g[:], w2_c[:], w2_s[:])
-            if late_out and not False and not (False and n in DIRECT):
+            if late_out and not False and not (True and n in DIRECT):
                 st_out(n - 2)
             if has(n - 1) and n - 1 >= N_UNITS - 1:
                 st_out(n - 1)

from contextlib import ExitStack

import concourse.mybir as mybir
from concourse.masks import make_identity

F32 = mybir.dt.float32
BF16 = mybir.dt.bfloat16
U32 = mybir.dt.uint32
U8 = mybir.dt.uint8
FP8X4 = mybir.dt.float8_e4m3fn_x4
RELU = mybir.ActivationFunctionType.Relu
ADD = mybir.AluOpType.add
MULT = mybir.AluOpType.mult

P = 128
B, D_IN, HID, OUT = 8192, 512, 512, 128
GROUP = 512
N_GROUPS = B // GROUP
FLOPS = 2 * B * D_IN * HID + 2 * B * (D_IN + HID) * OUT

VECTOR_TAKES = ((0,1),(2,0),(2,1))
LAST = (256,256)
DIRECT = (3,9)
SREGROUP = (16,)
GREGROUP = (2,8)
GPARTS = 1
GSHARE = 256
EX = ()
SHARED = tuple(n - 1 for n in EX) if GSHARE else ()
UNITS = [(g, 0, GROUP) for g in range(N_GROUPS - 1)] + [(N_GROUPS - 1, sum(LAST[:k]), LAST[k]) for k in range(len(LAST))]


def tile_dpn_t_kernel(tc, x, W1, b1, W2, b2, out):
    nc = tc.nc
    with ExitStack() as ctx:
        const = ctx.enter_context(tc.tile_pool(name="const", bufs=1))
        xin = ctx.enter_context(tc.tile_pool(name="xin", bufs=1))
        work = ctx.enter_context(tc.tile_pool(name="work", bufs=4))
        codes_pool = ctx.enter_context(tc.tile_pool(name="codes", bufs=7))
        outp = ctx.enter_context(tc.tile_pool(name="outp", bufs=8))
        psum = ctx.enter_context(tc.psum_pool(name="psum", bufs=1))
        ctx.enter_context(tc.manual_schedule())

        ident = const.tile([P, P], F32, name="ident")
        make_identity(nc, ident[:])

        x_sb = [xin.tile([P, 4, D_IN], BF16, name="x%d" % g) for g in range(N_GROUPS)]
        w1_sb = const.tile([P, 4, D_IN], BF16, name="w1_sb")
        w2_sb = const.tile([P, D_IN + HID], BF16, name="w2_sb")
        b1_raw = const.tile([P, 4], BF16, name="b1_raw")
        b1_f = const.tile([P, 4], F32, name="b1_f")
        b2_raw = const.tile([P, OUT], BF16, name="b2_raw")
        b2_f = const.tile([P, OUT], F32, name="b2_f")
        hold_h = const.tile([P, 1], BF16, name="hold_h")
        hold = const.tile([P, 1], U32, name="hold")

        def load_x(g, first, count):
            rows = x[g * GROUP : (g + 1) * GROUP, :].rearrange("(p j) k -> p j k", j=4)
            slots = slice(first, first + count)
            nc.sync.dma_start(out=x_sb[g][:, slots, :], in_=rows[:, slots, :])

        w1_rows = W1.rearrange("(p t) k -> p t k", t=4)

        warm = const.tile([P, 1], F32, name="warm")
        nc.vector.memset(warm[:], 0.0)
        nc.scalar.activation(out=warm[:], in_=warm[:], func=RELU)
        load_x(0, 0, 2)
        load_x(0, 2, 2)
        nc.sync.dma_start(out=w1_sb[:, 0:2, :], in_=w1_rows[:, 0:2, :])
        nc.sync.dma_start(out=w1_sb[:, 2:4, :], in_=w1_rows[:, 2:4, :])
        nc.sync.dma_start(out=b1_raw[:], in_=b1.rearrange("(p t) -> p t", t=4))
        load_x(1, 0, 2)
        load_x(1, 2, 2)
        load_x(2, 0, 2)
        load_x(2, 2, 2)
        nc.sync.dma_start(out=w2_sb[:], in_=W2)
        load_x(3, 0, 4)
        load_x(4, 0, 4)
        load_x(5, 0, 4)
        load_x(6, 0, 4)
        nc.sync.dma_start(out=b2_raw[:], in_=b2.partition_broadcast(P))
        for g in range(7, N_GROUPS):
            load_x(g, 0, 4)
        nc.gpsimd.tensor_copy(out=b1_f[:], in_=b1_raw[:])
        nc.gpsimd.tensor_copy(out=b2_f[:], in_=b2_raw[:])

        w1_g = const.tile([P, HID, 4], BF16, name="w1_g", align_bytes=64)
        w1_c = const.tile([P, HID], U32, name="w1_c", align_bytes=64)
        w1_s = const.tile([P, HID], U8, name="w1_s", align_bytes=64)
        w2_g = const.tile([P, 2 * OUT, 4], BF16, name="w2_g", align_bytes=64)
        w2_c = const.tile([P, 2 * OUT], U32, name="w2_c", align_bytes=64)
        w2_s = const.tile([P, 2 * OUT], U8, name="w2_s", align_bytes=64)

        live = {}

        def transpose_half(src, half, bank, slots=(0, 1)):
            words = src[:].bitcast(F32)
            for jj in slots:
                for u in range(2):
                    nc.tensor.transpose(
                        out=bank[:, jj, u, :],
                        in_=words[:, 2 * half + jj, u * P : (u + 1) * P],
                        identity=ident[:],
                    )

        def leave_bank(on_vector, bank, dst):
            dst = dst.bitcast(F32).rearrange("p (j r) u -> p j r u", j=2)
            src = bank[:].rearrange("p j u r -> p j r u")
            if on_vector:
                nc.vector.tensor_copy(out=dst, in_=src)
            else:
                nc.scalar.copy(out=dst, in_=src)

        def quantise(grouped, codes, scales):
            nc.vector.quantize_mx(
                out=codes.bitcast(FP8X4),
                scales=scales,
                in_=grouped.rearrange("p w j -> p (w j)"),
            )

        def has(n):
            return 0 <= n < len(UNITS)

        def st_transpose(g, half):
            bank = psum.tile([P, 2, 2, P], F32, name="x%d_%d" % (half, g), tag="x%d" % half)
            live[("x", g, half)] = bank
            transpose_half(x_sb[g], half, bank)

        def pair(m):
            if ("pair", m) not in live:
                x_width = GROUP if 0 <= m < N_GROUPS else 0
                h_width = UNITS[m - 3][2] if has(m - 3) else 0
                width = x_width + h_width
                live[("pair", m)] = work.tile([P, width, 4], BF16, name="pair%d" % m, tag="pair", align_bytes=64)
                live[("codes", m)] = codes_pool.tile([P, width], U32, name="c%d" % m, tag="c", align_bytes=64)
                live[("scales", m)] = codes_pool.tile([P, width], U8, name="s%d" % m, tag="s", align_bytes=64)
            return live[("pair", m)], (GROUP if m < N_GROUPS else 0)

        def st_leave_x(g, half):
            tile, h_first = pair(g)
            first = half * 2 * P
            leave_bank((g, half) in VECTOR_TAKES or g - 3 in EX, live[("x", g, half)], tile[:, first : first + 2 * P, :])

        def st_quantise(m):
            tile, h_first = pair(m)
            quantise(tile[:], live[("codes", m)][:], live[("scales", m)][:])

        def st_mm1(n, t):
            g, first, width = UNITS[n]
            if n in DIRECT:
                z = psum.tile([P, 4, P], F32, name="zd%d_%d" % (t, n), tag="z%d" % t)
                live[("z", n, t)] = z
                for tt in range(4):
                    nc.tensor.matmul_mx(
                        out=z[:, tt, :],
                        lhsT=w1_c[:, tt * P : (tt + 1) * P].bitcast(FP8X4),
                        lhsT_scale=w1_s[:, tt * P : (tt + 1) * P],
                        rhs=live[("codes", g)][:, t * P : (t + 1) * P].bitcast(FP8X4),
                        rhs_scale=live[("scales", g)][:, t * P : (t + 1) * P],
                        start=True,
                        stop=True,
                    )
                return
            cols = slice(first, first + width)
            z = psum.tile([P, width], F32, name="z%d_%d" % (t, n), tag="z%d" % t)
            live[("z", n, t)] = z
            nc.tensor.matmul_mx(
                out=z[:],
                lhsT=w1_c[:, t * P : (t + 1) * P].bitcast(FP8X4),
                lhsT_scale=w1_s[:, t * P : (t + 1) * P],
                rhs=live[("codes", g)][:, cols].bitcast(FP8X4),
                rhs_scale=live[("scales", g)][:, cols],
                start=True,
                stop=True,
            )

        def st_relu(n, t):
            width = UNITS[n][2]
            if n in DIRECT:
                tile, h_first = pair(n + 3)
                nc.vector.tensor_tensor(
                    out=tile[:, h_first + t * P : h_first + (t + 1) * P, :],
                    in0=live[("z", n, t)][:].rearrange("p t c -> p c t"),
                    in1=b1_f[:].unsqueeze(1).to_broadcast([P, P, 4]),
                    op=ADD,
                )
                return
            if ("hp", n) not in live:
                live[("hp", n)] = work.tile([P, 4, width], BF16, name="hp%d" % n, tag="hp")
            nc.scalar.activation(
                out=live[("hp", n)][:, t, :],
                in_=live[("z", n, t)][:],
                func=RELU,
                bias=b1_f[:, t : t + 1],
                scale=1.0,
            )

        def g_share(n):
            if n in GREGROUP:
                return UNITS[n][2]
            return GSHARE if n in SHARED and n not in DIRECT else 0

        def st_regroup(n):
            width = UNITS[n][2]
            tile, h_first = pair(n + 3)
            if n in DIRECT:
                whole = tile[:, h_first : h_first + width, :].rearrange("p c t -> p (c t)")
                nc.vector.tensor_scalar_max(out=whole, in0=whole, scalar1=0.0)
                return
            width -= g_share(n)
            if width == 0:
                return
            dst = tile[:, h_first : h_first + width, :].rearrange("p (c i) t -> p c t i", i=8)
            src = live[("hp", n)][:, :, :width].rearrange("p t (c i) -> p c t i", i=8)
            if n in SREGROUP:
                nc.scalar.copy(
                    out=tile[:, h_first : h_first + width, :],
                    in_=live[("hp", n)][:, :, :width].rearrange("p t c -> p c t"),
                )
            else:
                nc.vector.tensor_copy(out=dst, in_=src)

        def st_regroup_g(n):
            width = UNITS[n][2]
            share = g_share(n)
            if share == 0:
                return
            tile, h_first = pair(n + 3)
            if n in GREGROUP:
                nc.gpsimd.tensor_copy(out=hold[:], in_=live[("codes", n + 2)][:, 0:1])
            else:
                nc.gpsimd.tensor_copy(out=hold_h[:], in_=tile[:, h_first, 0:1])
            parts = GPARTS if n in GREGROUP else 1
            step = share // parts
            for k in range(parts):
                cols = slice(width - share + k * step, width - share + (k + 1) * step)
                nc.gpsimd.tensor_scalar(
                    out=tile[:, h_first + cols.start : h_first + cols.stop, :],
                    in0=live[("hp", n)][:, :, cols].rearrange("p t c -> p c t"),
                    scalar1=1.0,
                    scalar2=0.0,
                    op0=MULT,
                    op1=ADD,
                )

        def st_mm2(n):
            g, first, width = UNITS[n]
            h_first = pair(n + 3)[1]
            acc = psum.tile([P, width // P, OUT], F32, name="o%d" % n, tag="o", bufs=2)
            live[("o", n)] = acc
            for j in range(width // P):
                x_cols = slice(first + j * P, first + (j + 1) * P)
                h_cols = slice(h_first + j * P, h_first + (j + 1) * P)
                nc.tensor.matmul_mx(
                    out=acc[:, j, :],
                    lhsT=live[("codes", g)][:, x_cols].bitcast(FP8X4),
                    lhsT_scale=live[("scales", g)][:, x_cols],
                    rhs=w2_c[:, 0:OUT].bitcast(FP8X4),
                    rhs_scale=w2_s[:, 0:OUT],
                    start=True,
                    stop=False,
                )
                nc.tensor.matmul_mx(
                    out=acc[:, j, :],
                    lhsT=live[("codes", n + 3)][:, h_cols].bitcast(FP8X4),
                    lhsT_scale=live[("scales", n + 3)][:, h_cols],
                    rhs=w2_c[:, OUT : 2 * OUT].bitcast(FP8X4),
                    rhs_scale=w2_s[:, OUT : 2 * OUT],
                    start=False,
                    stop=True,
                )

        def st_out(n):
            g, first, width = UNITS[n]
            slots = slice(first // P, (first + width) // P)
            res = outp.tile([P, width // P, OUT], F32, name="res%d" % n, tag="res")
            nc.vector.tensor_tensor(
                out=res[:],
                in0=live[("o", n)][:],
                in1=b2_f[:].unsqueeze(1).to_broadcast([P, width // P, OUT]),
                op=ADD,
            )
            rows = out[g * GROUP : (g + 1) * GROUP, :].rearrange("(p j) o -> p j o", j=4)
            nc.sync.dma_start(out=rows[:, slots, :], in_=res[:])

        def prepare_w1(half, on_vector):
            bank = psum.tile([P, 2, 2, P], F32, name="w1b%d" % half, tag="z%d" % half)
            transpose_half(w1_sb, half, bank)
            leave_bank(on_vector, bank, w1_g[:, half * 2 * P : (half + 1) * 2 * P, :])

        def quantise_w1(half):
            cols = slice(half * 2 * P, (half + 1) * 2 * P)
            quantise(w1_g[:, cols, :], w1_c[:, cols], w1_s[:, cols])

        def transpose_w2():
            bank = psum.tile([P, 2, 2, P], F32, name="w2b", tag="o", bufs=2)
            live["w2b"] = bank
            words = w2_sb[:].bitcast(F32)
            for u in range(2):
                nc.tensor.transpose(out=bank[:, 0, u, :], in_=words[:, u * P : (u + 1) * P], identity=ident[:])
            for v in range(2):
                nc.tensor.transpose(out=bank[:, 1, v, :], in_=words[:, 2 * P + v : 4 * P : 2], identity=ident[:])

        def bring_slot(slot, tag, on_vector):
            bank = psum.tile([P, 2, P], F32, name="x0s%d" % slot, tag=tag)
            words = x_sb[0][:].bitcast(F32)
            for u in range(2):
                nc.tensor.transpose(out=bank[:, u, :], in_=words[:, slot, u * P : (u + 1) * P], identity=ident[:])
            dst = pair(0)[0][:, slot * P : (slot + 1) * P, :].rearrange("p c j -> p (c j)").bitcast(F32).rearrange("p (r u) -> p r u", u=2)
            src = bank[:].rearrange("p u r -> p r u")
            if on_vector:
                nc.vector.tensor_copy(out=dst, in_=src)
            else:
                nc.scalar.copy(out=dst, in_=src)

        def bring_w1(t):
            bank = psum.tile([P, 2, P], F32, name="w1q%d" % t, tag=("z0", "z1", "o", "o")[t], bufs=(1, 1, 2, 2)[t])
            words = w1_sb[:].bitcast(F32)
            for u in range(2):
                nc.tensor.transpose(out=bank[:, u, :], in_=words[:, t, u * P : (u + 1) * P], identity=ident[:])
            dst = w1_g[:, t * P : (t + 1) * P, :].rearrange("p c j -> p (c j)").bitcast(F32).rearrange("p (r u) -> p r u", u=2)
            src = bank[:].rearrange("p u r -> p r u")
            if t in ():
                nc.vector.tensor_copy(out=dst, in_=src)
            else:
                nc.scalar.copy(out=dst, in_=src)

        def quantise_w1q(first, count):
            cols = slice(first * P, (first + count) * P)
            quantise(w1_g[:, cols, :], w1_c[:, cols], w1_s[:, cols])

        def bring(g):
            for half in range(2):
                st_transpose(g, half)
                st_leave_x(g, half)

        N_UNITS = len(UNITS)
        bring(0)
        prepare_w1(0, 0 in ())
        st_quantise(0)
        quantise_w1(0)
        prepare_w1(1, 1 in ())
        quantise_w1(1)
        bring(1)
        for t in range(4):
            st_mm1(0, t)
        st_quantise(1)
        bring(2)
        transpose_w2()
        leave_bank(True, live["w2b"], w2_g[:])

        order = [0, 1, 2, 3]
        halves = [0, 1]
        for n in range(0, N_UNITS + 3):
            late_out = has(n - 2) and n - 2 < N_UNITS - 1
            if late_out and False:
                st_mm2(n - 2)
            if n + 3 < N_GROUPS:
                for half in halves:
                    st_transpose(n + 3, half)
            mm2_last = False and has(n + 1) and n not in DIRECT
            if late_out and not False and not mm2_last:
                st_mm2(n - 2)
            if late_out:
                if False:
                    st_out(n - 2)
            if n in DIRECT:
                for t in order:
                    st_relu(n, t)
                    if has(n + 1):
                        st_mm1(n + 1, t)
                if True:
                    st_out(n - 2)
                if True:
                    st_regroup(n)
            early = n in EX and n + 3 < N_GROUPS
            if early:
                for half in halves:
                    st_leave_x(n + 3, half)
            if n == 1 and not True:
                if not True:
                    transpose_w2()
                leave_bank(1, live["w2b"], w2_g[:])
            if n != 0 and (n + 2 < N_GROUPS or has(n - 1)):
                st_quantise(n + 2)
            if has(n - 1) and n - 1 >= N_UNITS - 1:
                st_mm2(n - 1)
            for t in order if n not in DIRECT else ():
                if has(n) and (n != 0 or not False):
                    st_relu(n, t)
                if has(n + 1):
                    st_mm1(n + 1, t)
            if late_out and not False and mm2_last:
                st_mm2(n - 2)
            if n + 3 < N_GROUPS:
                for half in halves:
                    if not early:
                        st_leave_x(n + 3, half)
            if has(n) and not (True and n in DIRECT):
                st_regroup(n)
                st_regroup_g(n)
            if n == 0:
                st_quantise(2)
            if True and not True and n == 1 - 1:
                transpose_w2()
            if n == 1:
                quantise(w2_g[:], w2_c[:], w2_s[:])
            if late_out and not False and not (True and n in DIRECT):
                st_out(n - 2)
            if has(n - 1) and n - 1 >= N_UNITS - 1:
                st_out(n - 1)
